import numpy as np
import ml_dtypes


def mxq(x, axis, fmt="e4m3"):
    dtype, down = {"e4m3": (ml_dtypes.float8_e4m3fn, 7), "e5m2": (ml_dtypes.float8_e5m2, 14)}[fmt]
    v = np.moveaxis(np.asarray(x, np.float32).astype(ml_dtypes.bfloat16).astype(np.float64), axis, -1)
    blocks = v.reshape(v.shape[:-1] + (-1, 32))
    amax = np.abs(blocks).max(-1, keepdims=True)
    byte = np.maximum(np.where(amax > 0, np.frexp(amax)[1] - 1 + 127, 0) - down, 1)
    scale = np.exp2(byte - 127.0)
    codes = (blocks / scale).astype(np.float32).astype(dtype).astype(np.float64)
    return np.moveaxis((codes * scale).reshape(v.shape), -1, axis)


BF16 = ml_dtypes.bfloat16


def bf(x):
    return np.asarray(x, np.float32).astype(BF16)


def f64(x):
    return np.asarray(x).astype(np.float64)


B, N, D, A = 32, 256, 512, 128
NB = N // A
EPS = 1e-12


def setup_inputs():
    e = np.random.standard_normal((B, N, D))
    g = np.random.standard_normal((B, N, 1))
    u = np.random.standard_normal((B, 1, D))
    amp = np.where(np.random.random((B, N, 1)) < 0.1, 0.25 * np.sqrt(EPS / D), 1.0)
    return {"data": bf(amp * (e + 2.0 * g * u))}


def reference(data):
    x = f64(data)
    sq = np.sum(x * x, axis=-1, keepdims=True)
    c = x * (1.0 / np.sqrt(np.maximum(sq, EPS)))
    cq = mxq(c, 2, "e4m3")
    sim = cq @ cq.transpose(0, 2, 1)
    sim = sim * np.tril(np.ones((N, N)))
    return sim.reshape(B, N, NB, A).mean(axis=-2)

@@ -1,0 +1,145 @@
+from contextlib import ExitStack
+
+import concourse.mybir as mybir
+from concourse.masks import make_identity
+
+FP8X4 = mybir.dt.float8_e4m3fn_x4
+BF16 = mybir.dt.bfloat16
+F32 = mybir.dt.float32
+U32 = mybir.dt.uint32
+U8 = mybir.dt.uint8
+ALU = mybir.AluOpType
+ACT = mybir.ActivationFunctionType
+
+B, N, D, A = 32, 256, 512, 128
+P = 128
+EPS = 1e-12
+HALF = D // 2
+RT = 4
+GB = 2
+
+FLOPS = 2 * B * N * N * D
+
+
+def tile_abstraction_pa_t_kernel(tc, data, out):
+    nc = tc.nc
+    with ExitStack() as ctx:
+        const = ctx.enter_context(tc.tile_pool(name="const", bufs=1))
+        xs = ctx.enter_context(tc.tile_pool(name="xs", bufs=1))
+        junkp = ctx.enter_context(tc.tile_pool(name="junkp", bufs=2))
+        small = ctx.enter_context(tc.tile_pool(name="small", bufs=4))
+        cp = ctx.enter_context(tc.tile_pool(name="cp", bufs=3))
+        gp = ctx.enter_context(tc.tile_pool(name="gp", bufs=3))
+        qp = ctx.enter_context(tc.tile_pool(name="qp", bufs=3))
+        op = ctx.enter_context(tc.tile_pool(name="op", bufs=3))
+        ps_t = ctx.enter_context(tc.psum_pool(name="ps_t", bufs=2))
+        ps_m = ctx.enter_context(tc.psum_pool(name="ps_m", bufs=3))
+        ps_s = ctx.enter_context(tc.psum_pool(name="ps_s", bufs=1))
+
+        rows = data.rearrange("b n (h c) -> (b n h) c", h=2)
+        sizes = [1, 1] + [2] * 15
+        x_of = []
+        b0 = 0
+        for i, nb in enumerate(sizes):
+            xt = xs.tile([P, RT * nb, HALF], BF16, name="x%d" % i)
+            nc.sync.dma_start(
+                out=xt[:],
+                in_=rows[b0 * 512 : (b0 + nb) * 512, :].rearrange("(t p) c -> p t c", p=P),
+            )
+            for k in range(nb):
+                x_of.append((xt, RT * k))
+            b0 += nb
+
+        warm = const.tile([P, 1], F32, name="warm")
+        nc.vector.memset(warm[:], 1.0)
+        nc.scalar.sqrt(out=warm[:], in_=warm[:])
+        ident_b = const.tile([P, P], BF16, name="ident_b")
+        make_identity(nc, ident_b[:])
+        ident_f = const.tile([P, P], F32, name="ident_f")
+        make_identity(nc, ident_f[:])
+        pair = const.tile([P, P], F32, name="pair")
+        idv = ident_f[:].rearrange("p (g j) -> p g j", j=2)
+        pav = pair[:].rearrange("p (g j) -> p g j", j=2)
+        for j in range(2):
+            nc.vector.tensor_tensor(out=pav[:, :, j], in0=idv[:, :, 0], in1=idv[:, :, 1], op=ALU.add)
+        mh = const.tile([P, A], F32, name="mh")
+        nc.gpsimd.memset(mh[:], 0.5)
+        nc.gpsimd.affine_select(
+            out=mh[:], in_=mh[:], compare_op=ALU.is_ge, fill=0.0, base=0,
+            pattern=[[-1, A]], channel_multiplier=1,
+        )
+
+        for g in range(B // GB):
+            ss = small.tile([P, RT * GB], F32, name="ss")
+            for i in range(GB):
+                xt, t0 = x_of[g * GB + i]
+                for t in range(RT):
+                    junk = junkp.tile([P, HALF], BF16, name="junk")
+                    nc.scalar.activation(
+                        out=junk[:], in_=xt[:, t0 + t, :], func=ACT.Square,
+                        accum_out=ss[:, RT * i + t : RT * i + t + 1],
+                    )
+            tot = ps_s.tile([P, RT * GB], F32, name="tot")
+            nc.tensor.matmul(out=tot[:], lhsT=pair[:], rhs=ss[:], start=True, stop=True)
+            fl = small.tile([P, RT * GB], F32, name="fl")
+            nc.vector.tensor_scalar_max(out=fl[:], in0=tot[:], scalar1=EPS)
+            rt = small.tile([P, RT * GB], F32, name="rt")
+            nc.scalar.sqrt(out=rt[:], in_=fl[:])
+            rinv = small.tile([P, RT * GB], F32, name="rinv")
+            nc.vector.reciprocal(out=rinv[:], in_=rt[:])
+
+            o = op.tile([P, 2 * GB, A], F32, name="o")
+            for i in range(GB):
+                xt, t0 = x_of[g * GB + i]
+                c = cp.tile([P, RT, HALF], BF16, name="c")
+                for t in range(RT):
+                    nc.vector.tensor_scalar_mul(
+                        out=c[:, t, :], in0=xt[:, t0 + t, :],
+                        scalar1=rinv[:, RT * i + t : RT * i + t + 1],
+                    )
+                grouped = gp.tile([P, 4 * N], BF16, name="grouped", align_bytes=64)
+                for u in range(2):
+                    pt = ps_t.tile([P, 4 * A], BF16, name="pt%d" % u)
+                    ptv = pt[:].rearrange("p (l q w h) -> p l q w h", l=2, q=64, w=2, h=2)
+                    for l in range(2):
+                        t = 2 * (1 - u) + l
+                        for w in range(2):
+                            nc.tensor.transpose(
+                                out=ptv[:, l, :, w, :],
+                                in_=c[:, t, w * P : (w + 1) * P],
+                                identity=ident_b[:],
+                            )
+                    if u == 0:
+                        nc.vector.tensor_copy(out=grouped[:, 0 : 4 * A], in_=pt[:])
+                    else:
+                        nc.scalar.copy(out=grouped[:, 4 * A : 8 * A], in_=pt[:])
+                codes = qp.tile([P, N], U32, name="codes", align_bytes=64)
+                sc = qp.tile([P, N], U8, name="sc", align_bytes=64)
+                nc.vector.quantize_mx(out=codes[:].bitcast(FP8X4), scales=sc[:], in_=grouped[:])
+                sim = ps_m.tile([P, 3 * A], F32, name="sim")
+                nc.tensor.matmul_mx(
+                    out=sim[:, A : 3 * A],
+                    lhsT=codes[:, 0:A].bitcast(FP8X4), lhsT_scale=sc[:, 0:A],
+                    rhs=codes[:, 0 : 2 * A].bitcast(FP8X4), rhs_scale=sc[:, 0 : 2 * A],
+                    start=True, stop=True,
+                )
+                nc.tensor.matmul_mx(
+                    out=sim[:, 0:A],
+                    lhsT=codes[:, A : 2 * A].bitcast(FP8X4), lhsT_scale=sc[:, A : 2 * A],
+                    rhs=codes[:, A : 2 * A].bitcast(FP8X4), rhs_scale=sc[:, A : 2 * A],
+                    start=True, stop=True,
+                )
+                nc.vector.tensor_tensor(
+                    out=o[:, 2 * i : 2 * i + 2, :],
+                    in0=sim[:, 0 : 2 * A].rearrange("p (r a) -> p r a", r=2),
+                    in1=mh[:].unsqueeze(1).to_broadcast([P, 2, A]),
+                    op=ALU.mult,
+                )
+                nc.vector.scalar_tensor_tensor(
+                    out=o[:, 2 * i + 1, :], in0=sim[:, 2 * A : 3 * A], scalar=0.5,
+                    in1=o[:, 2 * i + 1, :], op0=ALU.mult, op1=ALU.add,
+                )
+            nc.sync.dma_start(
+                out=out[g * GB : (g + 1) * GB].rearrange("g (r p) a -> p (g r) a", p=P),
+                in_=o[:],
+            )

@@ -14,9 +14,9 @@ ACT = mybir.ActivationFunctionType
 B, N, D, A = 32, 256, 512, 128
 P = 128
 EPS = 1e-12
-HALF = D // 2
-RT = 4
-GB = 2
+PAIRS = B // 2
+TILES = 4
+WORDS = D // 2
 
 FLOPS = 2 * B * N * N * D
 
@@ -26,120 +26,184 @@ def tile_abstraction_pa_t_kernel(tc, data, out):
     with ExitStack() as ctx:
         const = ctx.enter_context(tc.tile_pool(name="const", bufs=1))
         xs = ctx.enter_context(tc.tile_pool(name="xs", bufs=1))
-        junkp = ctx.enter_context(tc.tile_pool(name="junkp", bufs=2))
+        junkp = ctx.enter_context(tc.tile_pool(name="junkp", bufs=4))
         small = ctx.enter_context(tc.tile_pool(name="small", bufs=4))
         cp = ctx.enter_context(tc.tile_pool(name="cp", bufs=3))
         gp = ctx.enter_context(tc.tile_pool(name="gp", bufs=3))
         qp = ctx.enter_context(tc.tile_pool(name="qp", bufs=3))
-        op = ctx.enter_context(tc.tile_pool(name="op", bufs=3))
+        op = ctx.enter_context(tc.tile_pool(name="op", bufs=PAIRS))
         ps_t = ctx.enter_context(tc.psum_pool(name="ps_t", bufs=2))
-        ps_m = ctx.enter_context(tc.psum_pool(name="ps_m", bufs=3))
-        ps_s = ctx.enter_context(tc.psum_pool(name="ps_s", bufs=1))
+        ps_s = ctx.enter_context(tc.psum_pool(name="ps_s", bufs=2))
 
-        rows = data.rearrange("b n (h c) -> (b n h) c", h=2)
-        sizes = [1, 1] + [2] * 15
-        x_of = []
-        b0 = 0
-        for i, nb in enumerate(sizes):
-            xt = xs.tile([P, RT * nb, HALF], BF16, name="x%d" % i)
+        rows = data.rearrange("b n c -> (b n) c")
+        x_of = {}
+
+        def load(first, count):
+            xt = xs.tile([P, count, D], BF16, name="x%d" % first)
             nc.sync.dma_start(
                 out=xt[:],
-                in_=rows[b0 * 512 : (b0 + nb) * 512, :].rearrange("(t p) c -> p t c", p=P),
+                in_=rows[first * P : (first + count) * P, :].rearrange("(t p) c -> p t c", p=P),
             )
-            for k in range(nb):
-                x_of.append((xt, RT * k))
-            b0 += nb
+            for k in range(count):
+                x_of[first + k] = xt[:, k, :]
 
         warm = const.tile([P, 1], F32, name="warm")
         nc.vector.memset(warm[:], 1.0)
-        nc.scalar.sqrt(out=warm[:], in_=warm[:])
-        ident_b = const.tile([P, P], BF16, name="ident_b")
-        make_identity(nc, ident_b[:])
-        ident_f = const.tile([P, P], F32, name="ident_f")
-        make_identity(nc, ident_f[:])
-        pair = const.tile([P, P], F32, name="pair")
-        idv = ident_f[:].rearrange("p (g j) -> p g j", j=2)
-        pav = pair[:].rearrange("p (g j) -> p g j", j=2)
-        for j in range(2):
-            nc.vector.tensor_tensor(out=pav[:, :, j], in0=idv[:, :, 0], in1=idv[:, :, 1], op=ALU.add)
-        mh = const.tile([P, A], F32, name="mh")
-        nc.gpsimd.memset(mh[:], 0.5)
+        nc.scalar.activation(out=warm[:], in_=warm[:], func=ACT.Abs_reciprocal_sqrt)
+        ident = const.tile([P, P], F32, name="ident")
+        make_identity(nc, ident[:])
+        half = const.tile([P, A], F32, name="half")
+        nc.gpsimd.memset(half[:], 0.5)
         nc.gpsimd.affine_select(
-            out=mh[:], in_=mh[:], compare_op=ALU.is_ge, fill=0.0, base=0,
+            out=half[:], in_=half[:], compare_op=ALU.is_ge, fill=0.0, base=0,
             pattern=[[-1, A]], channel_multiplier=1,
         )
 
-        for g in range(B // GB):
-            ss = small.tile([P, RT * GB], F32, name="ss")
-            for i in range(GB):
-                xt, t0 = x_of[g * GB + i]
-                for t in range(RT):
-                    junk = junkp.tile([P, HALF], BF16, name="junk")
-                    nc.scalar.activation(
-                        out=junk[:], in_=xt[:, t0 + t, :], func=ACT.Square,
-                        accum_out=ss[:, RT * i + t : RT * i + t + 1],
-                    )
-            tot = ps_s.tile([P, RT * GB], F32, name="tot")
-            nc.tensor.matmul(out=tot[:], lhsT=pair[:], rhs=ss[:], start=True, stop=True)
-            fl = small.tile([P, RT * GB], F32, name="fl")
-            nc.vector.tensor_scalar_max(out=fl[:], in0=tot[:], scalar1=EPS)
-            rt = small.tile([P, RT * GB], F32, name="rt")
-            nc.scalar.sqrt(out=rt[:], in_=fl[:])
-            rinv = small.tile([P, RT * GB], F32, name="rinv")
-            nc.vector.reciprocal(out=rinv[:], in_=rt[:])
+        ctx.enter_context(tc.manual_schedule())
 
-            o = op.tile([P, 2 * GB, A], F32, name="o")
-            for i in range(GB):
-                xt, t0 = x_of[g * GB + i]
-                c = cp.tile([P, RT, HALF], BF16, name="c")
-                for t in range(RT):
-                    nc.vector.tensor_scalar_mul(
-                        out=c[:, t, :], in0=xt[:, t0 + t, :],
-                        scalar1=rinv[:, RT * i + t : RT * i + t + 1],
-                    )
-                grouped = gp.tile([P, 4 * N], BF16, name="grouped", align_bytes=64)
-                for u in range(2):
-                    pt = ps_t.tile([P, 4 * A], BF16, name="pt%d" % u)
-                    ptv = pt[:].rearrange("p (l q w h) -> p l q w h", l=2, q=64, w=2, h=2)
-                    for l in range(2):
-                        t = 2 * (1 - u) + l
-                        for w in range(2):
-                            nc.tensor.transpose(
-                                out=ptv[:, l, :, w, :],
-                                in_=c[:, t, w * P : (w + 1) * P],
-                                identity=ident_b[:],
-                            )
-                    if u == 0:
-                        nc.vector.tensor_copy(out=grouped[:, 0 : 4 * A], in_=pt[:])
-                    else:
-                        nc.scalar.copy(out=grouped[:, 4 * A : 8 * A], in_=pt[:])
-                codes = qp.tile([P, N], U32, name="codes", align_bytes=64)
-                sc = qp.tile([P, N], U8, name="sc", align_bytes=64)
-                nc.vector.quantize_mx(out=codes[:].bitcast(FP8X4), scales=sc[:], in_=grouped[:])
-                sim = ps_m.tile([P, 3 * A], F32, name="sim")
-                nc.tensor.matmul_mx(
-                    out=sim[:, A : 3 * A],
-                    lhsT=codes[:, 0:A].bitcast(FP8X4), lhsT_scale=sc[:, 0:A],
-                    rhs=codes[:, 0 : 2 * A].bitcast(FP8X4), rhs_scale=sc[:, 0 : 2 * A],
-                    start=True, stop=True,
-                )
-                nc.tensor.matmul_mx(
-                    out=sim[:, 0:A],
-                    lhsT=codes[:, A : 2 * A].bitcast(FP8X4), lhsT_scale=sc[:, A : 2 * A],
-                    rhs=codes[:, A : 2 * A].bitcast(FP8X4), rhs_scale=sc[:, A : 2 * A],
-                    start=True, stop=True,
-                )
-                nc.vector.tensor_tensor(
-                    out=o[:, 2 * i : 2 * i + 2, :],
-                    in0=sim[:, 0 : 2 * A].rearrange("p (r a) -> p r a", r=2),
-                    in1=mh[:].unsqueeze(1).to_broadcast([P, 2, A]),
-                    op=ALU.mult,
-                )
-                nc.vector.scalar_tensor_tensor(
-                    out=o[:, 2 * i + 1, :], in0=sim[:, 2 * A : 3 * A], scalar=0.5,
-                    in1=o[:, 2 * i + 1, :], op0=ALU.mult, op1=ALU.add,
-                )
-            nc.sync.dma_start(
-                out=out[g * GB : (g + 1) * GB].rearrange("g (r p) a -> p (g r) a", p=P),
-                in_=o[:],
+        load(0, 1)
+        load(1, 1)
+        load(2, 2)
+        for g in range(1, PAIRS):
+            load(TILES * g, TILES)
+
+        ss, rinv, cs, pts, gs, codes, scs, sims, hls, outs = {}, {}, {}, {}, {}, {}, {}, {}, {}, {}
+
+        def sums(g):
+            ss[g] = small.tile([P, TILES], F32, name="ss")
+
+        def square_s(g, t):
+            junk = junkp.tile([P, D], BF16, name="junk")
+            nc.scalar.activation(
+                out=junk[:], in_=x_of[TILES * g + t], func=ACT.Square,
+                accum_out=ss[g][:, t : t + 1],
             )
+
+        def square_v(g, t):
+            junkv = junkp.tile([P, D], BF16, name="junkv")
+            x = x_of[TILES * g + t]
+            nc.vector.scalar_tensor_tensor(
+                out=junkv[:], in0=x, scalar=1.0, in1=x, op0=ALU.mult, op1=ALU.mult,
+                accum_out=ss[g][:, t : t + 1],
+            )
+
+        def norm(g):
+            fl = small.tile([P, TILES], F32, name="fl")
+            nc.gpsimd.tensor_scalar_max(out=fl[:], in0=ss[g][:], scalar1=EPS)
+            rinv[g] = small.tile([P, TILES], F32, name="rinv")
+            nc.scalar.activation(out=rinv[g][:], in_=fl[:], func=ACT.Abs_reciprocal_sqrt)
+
+        def scale(g):
+            cs[g] = cp.tile([P, TILES, D], BF16, name="c")
+            for t in range(TILES):
+                nc.vector.tensor_scalar_mul(
+                    out=cs[g][:, t, :], in0=x_of[TILES * g + t], scalar1=rinv[g][:, t : t + 1]
+                )
+
+        def flip(g):
+            words = cs[g][:].rearrange("p t k -> p (t k)").bitcast(F32)
+            pts[g] = []
+            for b in range(2):
+                pt = ps_t.tile([P, 2, 2, P], F32, name="pt%d" % b)
+                for t in range(2):
+                    for u in range(2):
+                        w0 = (2 * b + t) * WORDS + u * P
+                        nc.tensor.transpose(
+                            out=pt[:, t, u, :], in_=words[:, w0 : w0 + P], identity=ident[:]
+                        )
+                pts[g].append(pt)
+
+        def group(g, b, copy):
+            if b == 0:
+                gs[g] = gp.tile([P, 2, 4 * N], BF16, name="grouped", align_bytes=64)
+            dst = gs[g][:, b, :].bitcast(F32).rearrange("p (t r u) -> p t r u", t=2, u=2)
+            copy(out=dst, in_=pts[g][b][:].rearrange("p t u r -> p t r u"))
+
+        def quantize(g):
+            codes[g] = qp.tile([P, 2 * N], U32, name="codes", align_bytes=64)
+            scs[g] = qp.tile([P, 2 * N], U8, name="sc", align_bytes=64)
+            nc.vector.quantize_mx(
+                out=codes[g][:].bitcast(FP8X4), scales=scs[g][:],
+                in_=gs[g][:].rearrange("p b k -> p (b k)"),
+            )
+
+        def multiply(g):
+            sims[g] = ps_s.tile([P, 4, A], F32, name="sim")
+            hls[g] = ps_s.tile([P, 2, A], F32, name="hl")
+
+            def mm(dst, i, j):
+                nc.tensor.matmul_mx(
+                    out=dst,
+                    lhsT=codes[g][:, i * A : (i + 1) * A].bitcast(FP8X4),
+                    lhsT_scale=scs[g][:, i * A : (i + 1) * A],
+                    rhs=codes[g][:, j * A : (j + 1) * A].bitcast(FP8X4),
+                    rhs_scale=scs[g][:, j * A : (j + 1) * A],
+                    start=True, stop=True,
+                )
+
+            for i in range(4):
+                mm(sims[g][:, i, :], i, i)
+            for b in range(2):
+                mm(hls[g][:, b, :], 2 * b + 1, 2 * b)
+
+        def mask(g):
+            outs[g] = op.tile([P, 4, A], F32, name="o")
+            nc.vector.tensor_tensor(
+                out=outs[g][:], in0=sims[g][:],
+                in1=half[:].unsqueeze(1).to_broadcast([P, 4, A]), op=ALU.mult,
+            )
+
+        def finish(g):
+            upper = outs[g][:].rearrange("p (b r) a -> p b r a", r=2)[:, :, 1, :]
+            nc.vector.scalar_tensor_tensor(
+                out=upper, in0=hls[g][:], scalar=0.5, in1=upper, op0=ALU.mult, op1=ALU.add
+            )
+            nc.sync.dma_start(
+                out=out[2 * g : 2 * g + 2].rearrange("g (r p) a -> p (g r) a", p=P),
+                in_=outs[g][:],
+            )
+
+        def scalar_step(s):
+            if s < PAIRS:
+                sums(s)
+                tiles = range(TILES)
+                if s == 0:
+                    tiles = (0, 2)
+                    square_v(0, 1)
+                    square_v(0, 3)
+                elif s == 1:
+                    tiles = (0, 1, 2)
+                    square_v(1, 3)
+                first = True
+                for t in tiles:
+                    square_s(s, t)
+                    if first and s >= 2:
+                        norm(s - 1)
+                    first = False
+                if s <= 0:
+                    norm(0)
+            elif s == PAIRS:
+                norm(s - 1)
+
+        def copy_b(g):
+            if g % 3 == 2 and g < PAIRS - 3:
+                return nc.vector.tensor_copy
+            return nc.scalar.copy
+
+        scalar_step(0)
+        scalar_step(1)
+        for v in range(PAIRS + 2):
+            scalar_step(v + 2)
+            if v < PAIRS:
+                scale(v)
+                flip(v)
+            if 1 <= v <= PAIRS:
+                quantize(v - 1)
+                multiply(v - 1)
+            if v >= 2:
+                mask(v - 2)
+            if v < PAIRS:
+                group(v, 0, nc.vector.tensor_copy)
+                group(v, 1, copy_b(v))
+            if v >= 2:
+                finish(v - 2)

@@ -141,6 +141,15 @@ def tile_abstraction_pa_t_kernel(tc, data, out):
                     start=True, stop=True,
                 )
 
+            wide = codes[max(g - 1, 0)], scs[max(g - 1, 0)]
+            for i in range(2):
+                nc.tensor.matmul_mx(
+                    out=sims[g][:].rearrange("p i a -> p (i a)"),
+                    lhsT=wide[0][:, i * A : (i + 1) * A].bitcast(FP8X4),
+                    lhsT_scale=wide[1][:, i * A : (i + 1) * A],
+                    rhs=wide[0][:].bitcast(FP8X4), rhs_scale=wide[1][:],
+                    start=True, stop=True,
+                )
             for i in range(4):
                 mm(sims[g][:, i, :], i, i)
             for b in range(2):

@@ -27,10 +27,10 @@ def tile_abstraction_pa_t_kernel(tc, data, out):
         const = ctx.enter_context(tc.tile_pool(name="const", bufs=1))
         xs = ctx.enter_context(tc.tile_pool(name="xs", bufs=1))
         junkp = ctx.enter_context(tc.tile_pool(name="junkp", bufs=4))
-        small = ctx.enter_context(tc.tile_pool(name="small", bufs=4))
-        cp = ctx.enter_context(tc.tile_pool(name="cp", bufs=3))
-        gp = ctx.enter_context(tc.tile_pool(name="gp", bufs=3))
-        qp = ctx.enter_context(tc.tile_pool(name="qp", bufs=3))
+        small = ctx.enter_context(tc.tile_pool(name="small", bufs=PAIRS))
+        cp = ctx.enter_context(tc.tile_pool(name="cp", bufs=4))
+        gp = ctx.enter_context(tc.tile_pool(name="gp", bufs=PAIRS))
+        qp = ctx.enter_context(tc.tile_pool(name="qp", bufs=4))
         op = ctx.enter_context(tc.tile_pool(name="op", bufs=PAIRS))
         ps_t = ctx.enter_context(tc.psum_pool(name="ps_t", bufs=2))
         ps_s = ctx.enter_context(tc.psum_pool(name="ps_s", bufs=2))
@@ -61,9 +61,8 @@ def tile_abstraction_pa_t_kernel(tc, data, out):
 
         ctx.enter_context(tc.manual_schedule())
 
-        load(0, 1)
-        load(1, 1)
-        load(2, 2)
+        for t in range(TILES):
+            load(t, 1)
         for g in range(1, PAIRS):
             load(TILES * g, TILES)
 
@@ -150,10 +149,10 @@ def tile_abstraction_pa_t_kernel(tc, data, out):
                     rhs=wide[0][:].bitcast(FP8X4), rhs_scale=wide[1][:],
                     start=True, stop=True,
                 )
-            for i in range(4):
-                mm(sims[g][:, i, :], i, i)
             for b in range(2):
                 mm(hls[g][:, b, :], 2 * b + 1, 2 * b)
+            for i in range(4):
+                mm(sims[g][:, i, :], i, i)
 
         def mask(g):
             outs[g] = op.tile([P, 4, A], F32, name="o")
@@ -172,47 +171,57 @@ def tile_abstraction_pa_t_kernel(tc, data, out):
                 in_=outs[g][:],
             )
 
-        def scalar_step(s):
-            if s < PAIRS:
-                sums(s)
-                tiles = range(TILES)
-                if s == 0:
-                    tiles = (0, 2)
-                    square_v(0, 1)
-                    square_v(0, 3)
-                elif s == 1:
-                    tiles = (0, 1, 2)
-                    square_v(1, 3)
-                first = True
-                for t in tiles:
-                    square_s(s, t)
-                    if first and s >= 2:
-                        norm(s - 1)
-                    first = False
-                if s <= 0:
-                    norm(0)
-            elif s == PAIRS:
-                norm(s - 1)
+        def copy_a(g):
+            if g >= PAIRS - 3 and g < PAIRS - 1:
+                return nc.scalar.copy
+            return nc.vector.tensor_copy
 
         def copy_b(g):
-            if g % 3 == 2 and g < PAIRS - 3:
+            if g % 3 == 2 and 0 < g < PAIRS - 3:
                 return nc.vector.tensor_copy
             return nc.scalar.copy
 
-        scalar_step(0)
-        scalar_step(1)
+        sums(0)
+        square_s(0, 0)
+        square_v(0, 1)
+        square_s(0, 2)
+        square_v(0, 3)
+        sums(1)
+        square_s(1, 0)
+        square_v(1, 1)
+        norm(0)
+        square_s(1, 2)
+        scale(0)
+        flip(0)
+        square_v(1, 3)
         for v in range(PAIRS + 2):
-            scalar_step(v + 2)
-            if v < PAIRS:
+            s = v + 2
+            if s < PAIRS:
+                sums(s)
+                square_s(s, 0)
+                square_s(s, 1)
+            if v + 1 < PAIRS:
+                norm(v + 1)
+            if 0 < v < PAIRS:
                 scale(v)
                 flip(v)
-            if 1 <= v <= PAIRS:
+            if v == PAIRS:
+                quantize(v - 1)
+                multiply(v - 1)
+                mask(v - 2)
+                mask(v - 1)
+                finish(v - 2)
+                finish(v - 1)
+                break
+            if v >= 1:
                 quantize(v - 1)
                 multiply(v - 1)
             if v >= 2:
                 mask(v - 2)
-            if v < PAIRS:
-                group(v, 0, nc.vector.tensor_copy)
-                group(v, 1, copy_b(v))
+            group(v, 0, copy_a(v))
+            group(v, 1, copy_b(v))
+            if s < PAIRS:
+                square_s(s, 2)
+                square_s(s, 3)
             if v >= 2:
                 finish(v - 2)

@@ -61,12 +61,15 @@ def tile_abstraction_pa_t_kernel(tc, data, out):
 
         ctx.enter_context(tc.manual_schedule())
 
-        for t in range(TILES):
+        for t in range(2 * TILES):
             load(t, 1)
-        for g in range(1, PAIRS):
-            load(TILES * g, TILES)
+        load(2 * TILES, TILES)
+        load(3 * TILES, TILES)
+        for g in range(4, PAIRS, 4):
+            load(TILES * g, 4 * TILES)
 
         ss, rinv, cs, pts, gs, codes, scs, sims, hls, outs = {}, {}, {}, {}, {}, {}, {}, {}, {}, {}
+        fls = {}
 
         def sums(g):
             ss[g] = small.tile([P, TILES], F32, name="ss")
@@ -86,11 +89,13 @@ def tile_abstraction_pa_t_kernel(tc, data, out):
                 accum_out=ss[g][:, t : t + 1],
             )
 
+        def floor(g, engine):
+            fls[g] = small.tile([P, TILES], F32, name="fl")
+            engine.tensor_scalar_max(out=fls[g][:], in0=ss[g][:], scalar1=EPS)
+
         def norm(g):
-            fl = small.tile([P, TILES], F32, name="fl")
-            nc.gpsimd.tensor_scalar_max(out=fl[:], in0=ss[g][:], scalar1=EPS)
             rinv[g] = small.tile([P, TILES], F32, name="rinv")
-            nc.scalar.activation(out=rinv[g][:], in_=fl[:], func=ACT.Abs_reciprocal_sqrt)
+            nc.scalar.activation(out=rinv[g][:], in_=fls[g][:], func=ACT.Abs_reciprocal_sqrt)
 
         def scale(g):
             cs[g] = cp.tile([P, TILES, D], BF16, name="c")
@@ -113,7 +118,7 @@ def tile_abstraction_pa_t_kernel(tc, data, out):
                 pts[g].append(pt)
 
         def group(g, b, copy):
-            if b == 0:
+            if g not in gs:
                 gs[g] = gp.tile([P, 2, 4 * N], BF16, name="grouped", align_bytes=64)
             dst = gs[g][:, b, :].bitcast(F32).rearrange("p (t r u) -> p t r u", t=2, u=2)
             copy(out=dst, in_=pts[g][b][:].rearrange("p t u r -> p t r u"))
@@ -141,7 +146,7 @@ def tile_abstraction_pa_t_kernel(tc, data, out):
                 )
 
             wide = codes[max(g - 1, 0)], scs[max(g - 1, 0)]
-            for i in range(2):
+            for i in range(2 if g < PAIRS - 1 else 0):
                 nc.tensor.matmul_mx(
                     out=sims[g][:].rearrange("p i a -> p (i a)"),
                     lhsT=wide[0][:, i * A : (i + 1) * A].bitcast(FP8X4),
@@ -166,62 +171,79 @@ def tile_abstraction_pa_t_kernel(tc, data, out):
             nc.vector.scalar_tensor_tensor(
                 out=upper, in0=hls[g][:], scalar=0.5, in1=upper, op0=ALU.mult, op1=ALU.add
             )
-            nc.sync.dma_start(
-                out=out[2 * g : 2 * g + 2].rearrange("g (r p) a -> p (g r) a", p=P),
-                in_=outs[g][:],
-            )
+
+        def store(g, r=None):
+            dst = out[2 * g : 2 * g + 2].rearrange("g (r p) a -> p g r a", p=P)
+            src = outs[g][:].rearrange("p (g r) a -> p g r a", r=2)
+            if r is not None:
+                dst, src = dst[:, :, r, :], src[:, :, r, :]
+            nc.sync.dma_start(out=dst, in_=src)
 
         def copy_a(g):
-            if g >= PAIRS - 3 and g < PAIRS - 1:
-                return nc.scalar.copy
-            return nc.vector.tensor_copy
+            return nc.scalar.copy if g >= PAIRS - 2 else nc.vector.tensor_copy
 
         def copy_b(g):
-            if g % 3 == 2 and 0 < g < PAIRS - 3:
-                return nc.vector.tensor_copy
-            return nc.scalar.copy
+            return nc.vector.tensor_copy if g % 4 == 3 and g < 13 else nc.scalar.copy
+
+        def on_vector(s, t):
+            return t == 3 and s == 2
+
+        def square_scalar(s, tiles):
+            for t in tiles:
+                if not on_vector(s, t):
+                    square_s(s, t)
+
+        def square_vector(s):
+            for t in range(TILES):
+                if on_vector(s, t):
+                    square_v(s, t)
 
         sums(0)
-        square_s(0, 0)
-        square_v(0, 1)
-        square_s(0, 2)
-        square_v(0, 3)
         sums(1)
+        square_s(0, 0)
+        square_s(0, 2)
         square_s(1, 0)
-        square_v(1, 1)
+        square_v(0, 1)
+        square_v(0, 3)
+        floor(0, nc.vector)
         norm(0)
         square_s(1, 2)
+        square_v(1, 1)
         scale(0)
         flip(0)
         square_v(1, 3)
-        for v in range(PAIRS + 2):
+        floor(1, nc.vector)
+        for v in range(PAIRS + 1):
             s = v + 2
             if s < PAIRS:
                 sums(s)
-                square_s(s, 0)
-                square_s(s, 1)
+                square_scalar(s, range(2))
+            if 2 <= v + 1 < PAIRS:
+                floor(v + 1, nc.gpsimd)
             if v + 1 < PAIRS:
                 norm(v + 1)
             if 0 < v < PAIRS:
                 scale(v)
                 flip(v)
-            if v == PAIRS:
-                quantize(v - 1)
-                multiply(v - 1)
-                mask(v - 2)
-                mask(v - 1)
-                finish(v - 2)
-                finish(v - 1)
-                break
             if v >= 1:
                 quantize(v - 1)
                 multiply(v - 1)
             if v >= 2:
                 mask(v - 2)
+            if s < PAIRS:
+                square_vector(s)
+            if v == PAIRS:
+                mask(v - 1)
+                store(v - 1, 0)
+                finish(v - 2)
+                store(v - 2)
+                finish(v - 1)
+                store(v - 1, 1)
+                break
             group(v, 0, copy_a(v))
             group(v, 1, copy_b(v))
             if s < PAIRS:
-                square_s(s, 2)
-                square_s(s, 3)
+                square_scalar(s, range(2, TILES))
             if v >= 2:
                 finish(v - 2)
+                store(v - 2)

@@ -15,6 +15,7 @@ B, N, D, A = 32, 256, 512, 128
 P = 128
 EPS = 1e-12
 PAIRS = B // 2
+LAST = PAIRS - 1
 TILES = 4
 WORDS = D // 2
 
@@ -28,10 +29,10 @@ def tile_abstraction_pa_t_kernel(tc, data, out):
         xs = ctx.enter_context(tc.tile_pool(name="xs", bufs=1))
         junkp = ctx.enter_context(tc.tile_pool(name="junkp", bufs=4))
         small = ctx.enter_context(tc.tile_pool(name="small", bufs=PAIRS))
-        cp = ctx.enter_context(tc.tile_pool(name="cp", bufs=4))
         gp = ctx.enter_context(tc.tile_pool(name="gp", bufs=PAIRS))
-        qp = ctx.enter_context(tc.tile_pool(name="qp", bufs=4))
         op = ctx.enter_context(tc.tile_pool(name="op", bufs=PAIRS))
+        cp = ctx.enter_context(tc.tile_pool(name="cp", bufs=4))
+        qp = ctx.enter_context(tc.tile_pool(name="qp", bufs=4))
         ps_t = ctx.enter_context(tc.psum_pool(name="ps_t", bufs=2))
         ps_s = ctx.enter_context(tc.psum_pool(name="ps_s", bufs=2))
 
@@ -63,15 +64,14 @@ def tile_abstraction_pa_t_kernel(tc, data, out):
 
         for t in range(2 * TILES):
             load(t, 1)
-        load(2 * TILES, TILES)
-        load(3 * TILES, TILES)
-        for g in range(4, PAIRS, 4):
-            load(TILES * g, 4 * TILES)
+        load(2 * TILES, 2)
+        load(2 * TILES + 2, 2)
+        for g in range(3, PAIRS):
+            load(TILES * g, TILES)
 
-        ss, rinv, cs, pts, gs, codes, scs, sims, hls, outs = {}, {}, {}, {}, {}, {}, {}, {}, {}, {}
-        fls = {}
+        ss, fls, rinv, cs, pts, gs, codes, scs, sims, hls, outs = {}, {}, {}, {}, {}, {}, {}, {}, {}, {}, {}
 
-        def sums(g):
+        def new_sums(g):
             ss[g] = small.tile([P, TILES], F32, name="ss")
 
         def square_s(g, t):
@@ -117,53 +117,47 @@ def tile_abstraction_pa_t_kernel(tc, data, out):
                         )
                 pts[g].append(pt)
 
-        def group(g, b, copy):
+        def gather(g, b, copy):
             if g not in gs:
                 gs[g] = gp.tile([P, 2, 4 * N], BF16, name="grouped", align_bytes=64)
             dst = gs[g][:, b, :].bitcast(F32).rearrange("p (t r u) -> p t r u", t=2, u=2)
             copy(out=dst, in_=pts[g][b][:].rearrange("p t u r -> p t r u"))
 
-        def quantize(g):
-            codes[g] = qp.tile([P, 2 * N], U32, name="codes", align_bytes=64)
-            scs[g] = qp.tile([P, 2 * N], U8, name="sc", align_bytes=64)
+        def quantize(g, batches):
+            if g not in codes:
+                codes[g] = qp.tile([P, 2 * N], U32, name="codes", align_bytes=64)
+                scs[g] = qp.tile([P, 2 * N], U8, name="sc", align_bytes=64)
+            cols = slice(batches.start * N, batches.stop * N)
             nc.vector.quantize_mx(
-                out=codes[g][:].bitcast(FP8X4), scales=scs[g][:],
-                in_=gs[g][:].rearrange("p b k -> p (b k)"),
+                out=codes[g][:, cols].bitcast(FP8X4), scales=scs[g][:, cols],
+                in_=gs[g][:, batches, :].rearrange("p b k -> p (b k)"),
+            )
+
+        def product(dst, g, i, cols):
+            nc.tensor.matmul_mx(
+                out=dst,
+                lhsT=codes[g][:, i * A : (i + 1) * A].bitcast(FP8X4),
+                lhsT_scale=scs[g][:, i * A : (i + 1) * A],
+                rhs=codes[g][:, cols].bitcast(FP8X4), rhs_scale=scs[g][:, cols],
+                start=True, stop=True,
             )
 
         def multiply(g):
-            sims[g] = ps_s.tile([P, 4, A], F32, name="sim")
+            sims[g] = ps_s.tile([P, TILES, A], F32, name="sim")
             hls[g] = ps_s.tile([P, 2, A], F32, name="hl")
-
-            def mm(dst, i, j):
-                nc.tensor.matmul_mx(
-                    out=dst,
-                    lhsT=codes[g][:, i * A : (i + 1) * A].bitcast(FP8X4),
-                    lhsT_scale=scs[g][:, i * A : (i + 1) * A],
-                    rhs=codes[g][:, j * A : (j + 1) * A].bitcast(FP8X4),
-                    rhs_scale=scs[g][:, j * A : (j + 1) * A],
-                    start=True, stop=True,
-                )
-
-            wide = codes[max(g - 1, 0)], scs[max(g - 1, 0)]
-            for i in range(2 if g < PAIRS - 1 else 0):
-                nc.tensor.matmul_mx(
-                    out=sims[g][:].rearrange("p i a -> p (i a)"),
-                    lhsT=wide[0][:, i * A : (i + 1) * A].bitcast(FP8X4),
-                    lhsT_scale=wide[1][:, i * A : (i + 1) * A],
-                    rhs=wide[0][:].bitcast(FP8X4), rhs_scale=wide[1][:],
-                    start=True, stop=True,
-                )
+            if g < LAST:
+                for i in range(2):
+                    product(sims[g][:].rearrange("p i a -> p (i a)"), max(g - 1, 0), i, slice(0, 2 * N))
             for b in range(2):
-                mm(hls[g][:, b, :], 2 * b + 1, 2 * b)
-            for i in range(4):
-                mm(sims[g][:, i, :], i, i)
+                product(hls[g][:, b, :], g, 2 * b + 1, slice(2 * b * A, (2 * b + 1) * A))
+            for i in range(TILES):
+                product(sims[g][:, i, :], g, i, slice(i * A, (i + 1) * A))
 
         def mask(g):
-            outs[g] = op.tile([P, 4, A], F32, name="o")
+            outs[g] = op.tile([P, TILES, A], F32, name="o")
             nc.vector.tensor_tensor(
                 out=outs[g][:], in0=sims[g][:],
-                in1=half[:].unsqueeze(1).to_broadcast([P, 4, A]), op=ALU.mult,
+                in1=half[:].unsqueeze(1).to_broadcast([P, TILES, A]), op=ALU.mult,
             )
 
         def finish(g):
@@ -172,34 +166,15 @@ def tile_abstraction_pa_t_kernel(tc, data, out):
                 out=upper, in0=hls[g][:], scalar=0.5, in1=upper, op0=ALU.mult, op1=ALU.add
             )
 
-        def store(g, r=None):
+        def store(g, halves=slice(0, 2)):
             dst = out[2 * g : 2 * g + 2].rearrange("g (r p) a -> p g r a", p=P)
             src = outs[g][:].rearrange("p (g r) a -> p g r a", r=2)
-            if r is not None:
-                dst, src = dst[:, :, r, :], src[:, :, r, :]
-            nc.sync.dma_start(out=dst, in_=src)
+            nc.sync.dma_start(out=dst[:, :, halves, :], in_=src[:, :, halves, :])
 
-        def copy_a(g):
-            return nc.scalar.copy if g >= PAIRS - 2 else nc.vector.tensor_copy
+        first, second, both = slice(0, 1), slice(1, 2), slice(0, 2)
 
-        def copy_b(g):
-            return nc.vector.tensor_copy if g % 4 == 3 and g < 13 else nc.scalar.copy
-
-        def on_vector(s, t):
-            return t == 3 and s == 2
-
-        def square_scalar(s, tiles):
-            for t in tiles:
-                if not on_vector(s, t):
-                    square_s(s, t)
-
-        def square_vector(s):
-            for t in range(TILES):
-                if on_vector(s, t):
-                    square_v(s, t)
-
-        sums(0)
-        sums(1)
+        new_sums(0)
+        new_sums(1)
         square_s(0, 0)
         square_s(0, 2)
         square_s(1, 0)
@@ -213,37 +188,49 @@ def tile_abstraction_pa_t_kernel(tc, data, out):
         flip(0)
         square_v(1, 3)
         floor(1, nc.vector)
-        for v in range(PAIRS + 1):
+
+        for v in range(PAIRS):
             s = v + 2
             if s < PAIRS:
-                sums(s)
-                square_scalar(s, range(2))
-            if 2 <= v + 1 < PAIRS:
+                new_sums(s)
+                square_s(s, 0)
+                square_s(s, 1)
+            if 1 <= v < LAST:
                 floor(v + 1, nc.gpsimd)
-            if v + 1 < PAIRS:
+            if v < LAST - 1:
                 norm(v + 1)
-            if 0 < v < PAIRS:
+            if v > 0:
                 scale(v)
                 flip(v)
-            if v >= 1:
-                quantize(v - 1)
+                quantize(v - 1, both)
                 multiply(v - 1)
             if v >= 2:
                 mask(v - 2)
+            if v == 0:
+                square_v(2, 3)
+            if v < LAST - 1:
+                gather(v, 0, nc.vector.tensor_copy)
+                gather(v, 1, nc.vector.tensor_copy if v % 4 == 3 else nc.scalar.copy)
+            else:
+                gather(v, 0, nc.scalar.copy)
+                if v == LAST - 1:
+                    norm(LAST)
+                gather(v, 1, nc.scalar.copy)
             if s < PAIRS:
-                square_vector(s)
-            if v == PAIRS:
-                mask(v - 1)
-                store(v - 1, 0)
-                finish(v - 2)
-                store(v - 2)
-                finish(v - 1)
-                store(v - 1, 1)
-                break
-            group(v, 0, copy_a(v))
-            group(v, 1, copy_b(v))
-            if s < PAIRS:
-                square_scalar(s, range(2, TILES))
+                square_s(s, 2)
+                if s > 2:
+                    square_s(s, 3)
             if v >= 2:
                 finish(v - 2)
                 store(v - 2)
+
+        quantize(LAST, first)
+        quantize(LAST, second)
+        multiply(LAST)
+        mask(LAST - 1)
+        mask(LAST)
+        store(LAST, first)
+        finish(LAST - 1)
+        store(LAST - 1)
+        finish(LAST)
+        store(LAST, second)

from contextlib import ExitStack

import concourse.mybir as mybir
from concourse.masks import make_identity

FP8X4 = mybir.dt.float8_e4m3fn_x4
BF16 = mybir.dt.bfloat16
F32 = mybir.dt.float32
U32 = mybir.dt.uint32
U8 = mybir.dt.uint8
ALU = mybir.AluOpType
ACT = mybir.ActivationFunctionType

B, N, D, A = 32, 256, 512, 128
P = 128
EPS = 1e-12
PAIRS = B // 2
LAST = PAIRS - 1
TILES = 4
WORDS = D // 2

FLOPS = 2 * B * N * N * D


def tile_abstraction_pa_t_kernel(tc, data, out):
    nc = tc.nc
    with ExitStack() as ctx:
        const = ctx.enter_context(tc.tile_pool(name="const", bufs=1))
        xs = ctx.enter_context(tc.tile_pool(name="xs", bufs=1))
        junkp = ctx.enter_context(tc.tile_pool(name="junkp", bufs=4))
        small = ctx.enter_context(tc.tile_pool(name="small", bufs=PAIRS))
        gp = ctx.enter_context(tc.tile_pool(name="gp", bufs=PAIRS))
        op = ctx.enter_context(tc.tile_pool(name="op", bufs=PAIRS))
        cp = ctx.enter_context(tc.tile_pool(name="cp", bufs=4))
        qp = ctx.enter_context(tc.tile_pool(name="qp", bufs=4))
        ps_t = ctx.enter_context(tc.psum_pool(name="ps_t", bufs=2))
        ps_s = ctx.enter_context(tc.psum_pool(name="ps_s", bufs=2))

        rows = data.rearrange("b n c -> (b n) c")
        x_of = {}

        def load(first, count):
            xt = xs.tile([P, count, D], BF16, name="x%d" % first)
            nc.sync.dma_start(
                out=xt[:],
                in_=rows[first * P : (first + count) * P, :].rearrange("(t p) c -> p t c", p=P),
            )
            for k in range(count):
                x_of[first + k] = xt[:, k, :]

        warm = const.tile([P, 1], F32, name="warm")
        nc.vector.memset(warm[:], 1.0)
        nc.scalar.activation(out=warm[:], in_=warm[:], func=ACT.Abs_reciprocal_sqrt)
        ident = const.tile([P, P], F32, name="ident")
        make_identity(nc, ident[:])
        half = const.tile([P, A], F32, name="half")
        nc.gpsimd.memset(half[:], 0.5)
        nc.gpsimd.affine_select(
            out=half[:], in_=half[:], compare_op=ALU.is_ge, fill=0.0, base=0,
            pattern=[[-1, A]], channel_multiplier=1,
        )

        ctx.enter_context(tc.manual_schedule())

        for t in range(2 * TILES):
            load(t, 1)
        load(2 * TILES, 2)
        load(2 * TILES + 2, 2)
        for g in range(3, PAIRS):
            load(TILES * g, TILES)

        ss, fls, rinv, cs, pts, gs, codes, scs, sims, hls, outs = {}, {}, {}, {}, {}, {}, {}, {}, {}, {}, {}

        def new_sums(g):
            ss[g] = small.tile([P, TILES], F32, name="ss")

        def square_s(g, t):
            junk = junkp.tile([P, D], BF16, name="junk")
            nc.scalar.activation(
                out=junk[:], in_=x_of[TILES * g + t], func=ACT.Square,
                accum_out=ss[g][:, t : t + 1],
            )

        def square_v(g, t):
            junkv = junkp.tile([P, D], BF16, name="junkv")
            x = x_of[TILES * g + t]
            nc.vector.scalar_tensor_tensor(
                out=junkv[:], in0=x, scalar=1.0, in1=x, op0=ALU.mult, op1=ALU.mult,
                accum_out=ss[g][:, t : t + 1],
            )

        def floor(g, engine):
            fls[g] = small.tile([P, TILES], F32, name="fl")
            engine.tensor_scalar_max(out=fls[g][:], in0=ss[g][:], scalar1=EPS)

        def norm(g):
            rinv[g] = small.tile([P, TILES], F32, name="rinv")
            nc.scalar.activation(out=rinv[g][:], in_=fls[g][:], func=ACT.Abs_reciprocal_sqrt)

        def scale(g):
            cs[g] = cp.tile([P, TILES, D], BF16, name="c")
            for t in range(TILES):
                nc.vector.tensor_scalar_mul(
                    out=cs[g][:, t, :], in0=x_of[TILES * g + t], scalar1=rinv[g][:, t : t + 1]
                )

        def flip(g):
            words = cs[g][:].rearrange("p t k -> p (t k)").bitcast(F32)
            pts[g] = []
            for b in range(2):
                pt = ps_t.tile([P, 2, 2, P], F32, name="pt%d" % b)
                for t in range(2):
                    for u in range(2):
                        w0 = (2 * b + t) * WORDS + u * P
                        nc.tensor.transpose(
                            out=pt[:, t, u, :], in_=words[:, w0 : w0 + P], identity=ident[:]
                        )
                pts[g].append(pt)

        def gather(g, b, copy):
            if g not in gs:
                gs[g] = gp.tile([P, 2, 4 * N], BF16, name="grouped", align_bytes=64)
            dst = gs[g][:, b, :].bitcast(F32).rearrange("p (t r u) -> p t r u", t=2, u=2)
            copy(out=dst, in_=pts[g][b][:].rearrange("p t u r -> p t r u"))

        def quantize(g, batches):
            if g not in codes:
                codes[g] = qp.tile([P, 2 * N], U32, name="codes", align_bytes=64)
                scs[g] = qp.tile([P, 2 * N], U8, name="sc", align_bytes=64)
            cols = slice(batches.start * N, batches.stop * N)
            nc.vector.quantize_mx(
                out=codes[g][:, cols].bitcast(FP8X4), scales=scs[g][:, cols],
                in_=gs[g][:, batches, :].rearrange("p b k -> p (b k)"),
            )

        def product(dst, g, i, cols):
            nc.tensor.matmul_mx(
                out=dst,
                lhsT=codes[g][:, i * A : (i + 1) * A].bitcast(FP8X4),
                lhsT_scale=scs[g][:, i * A : (i + 1) * A],
                rhs=codes[g][:, cols].bitcast(FP8X4), rhs_scale=scs[g][:, cols],
                start=True, stop=True,
            )

        def multiply(g):
            sims[g] = ps_s.tile([P, TILES, A], F32, name="sim")
            hls[g] = ps_s.tile([P, 2, A], F32, name="hl")
            if g < LAST:
                for i in range(2):
                    product(sims[g][:].rearrange("p i a -> p (i a)"), max(g - 1, 0), i, slice(0, 2 * N))
            for b in range(2):
                product(hls[g][:, b, :], g, 2 * b + 1, slice(2 * b * A, (2 * b + 1) * A))
            for i in range(TILES):
                product(sims[g][:, i, :], g, i, slice(i * A, (i + 1) * A))

        def mask(g):
            outs[g] = op.tile([P, TILES, A], F32, name="o")
            nc.vector.tensor_tensor(
                out=outs[g][:], in0=sims[g][:],
                in1=half[:].unsqueeze(1).to_broadcast([P, TILES, A]), op=ALU.mult,
            )

        def finish(g):
            upper = outs[g][:].rearrange("p (b r) a -> p b r a", r=2)[:, :, 1, :]
            nc.vector.scalar_tensor_tensor(
                out=upper, in0=hls[g][:], scalar=0.5, in1=upper, op0=ALU.mult, op1=ALU.add
            )

        def store(g, halves=slice(0, 2)):
            dst = out[2 * g : 2 * g + 2].rearrange("g (r p) a -> p g r a", p=P)
            src = outs[g][:].rearrange("p (g r) a -> p g r a", r=2)
            nc.sync.dma_start(out=dst[:, :, halves, :], in_=src[:, :, halves, :])

        first, second, both = slice(0, 1), slice(1, 2), slice(0, 2)

        new_sums(0)
        new_sums(1)
        square_s(0, 0)
        square_s(0, 2)
        square_s(1, 0)
        square_v(0, 1)
        square_v(0, 3)
        floor(0, nc.vector)
        norm(0)
        square_s(1, 2)
        square_v(1, 1)
        scale(0)
        flip(0)
        square_v(1, 3)
        floor(1, nc.vector)

        for v in range(PAIRS):
            s = v + 2
            if s < PAIRS:
                new_sums(s)
                square_s(s, 0)
                square_s(s, 1)
            if 1 <= v < LAST:
                floor(v + 1, nc.gpsimd)
            if v < LAST - 1:
                norm(v + 1)
            if v > 0:
                scale(v)
                flip(v)
                quantize(v - 1, both)
                multiply(v - 1)
            if v >= 2:
                mask(v - 2)
            if v == 0:
                square_v(2, 3)
            if v < LAST - 1:
                gather(v, 0, nc.vector.tensor_copy)
                gather(v, 1, nc.vector.tensor_copy if v % 4 == 3 else nc.scalar.copy)
            else:
                gather(v, 0, nc.scalar.copy)
                if v == LAST - 1:
                    norm(LAST)
                gather(v, 1, nc.scalar.copy)
            if s < PAIRS:
                square_s(s, 2)
                if s > 2:
                    square_s(s, 3)
            if v >= 2:
                finish(v - 2)
                store(v - 2)

        quantize(LAST, first)
        quantize(LAST, second)
        multiply(LAST)
        mask(LAST - 1)
        mask(LAST)
        store(LAST, first)
        finish(LAST - 1)
        store(LAST - 1)
        finish(LAST)
        store(LAST, second)
